import numpy as np
import ml_dtypes


def mxq(x, axis, fmt="e4m3"):
    dtype, down = {"e4m3": (ml_dtypes.float8_e4m3fn, 7), "e5m2": (ml_dtypes.float8_e5m2, 14)}[fmt]
    v = np.moveaxis(np.asarray(x, np.float32).astype(ml_dtypes.bfloat16).astype(np.float64), axis, -1)
    blocks = v.reshape(v.shape[:-1] + (-1, 32))
    amax = np.abs(blocks).max(-1, keepdims=True)
    byte = np.maximum(np.where(amax > 0, np.frexp(amax)[1] - 1 + 127, 0) - down, 1)
    scale = np.exp2(byte - 127.0)
    codes = (blocks / scale).astype(np.float32).astype(dtype).astype(np.float64)
    return np.moveaxis((codes * scale).reshape(v.shape), -1, axis)


WIDE = False


def mx_kscale(k):
    if not WIDE:
        return np.ones(k)
    levels = np.array([10, -10, 5, -5, 0])
    if k % 512:
        return np.exp2(np.random.permutation(np.resize(levels, k // 32))).repeat(32)
    a = np.empty((k // 512, 16))
    for p in range(k // 512):
        a[p, :8] = np.random.permutation(np.resize(levels, 8))
        for g in range(8):
            far = levels[np.abs(levels - a[p, g]) >= 10]
            a[p, g + 8] = far[np.random.randint(len(far))]
    return np.exp2(a.ravel()).repeat(32)


BF16 = ml_dtypes.bfloat16


def bf(x):
    return np.asarray(x, np.float32).astype(BF16)


def f64(x):
    return np.asarray(x).astype(np.float64)


B, S, E, H, DH, ROT, MP = 2, 512, 1024, 8, 128, 32, 4
HD = H * DH
LOC = HD // MP


def rope_sincos():
    inv_freq = 1.0 / (10000.0 ** (np.arange(0, ROT, 2) / ROT))
    ang = np.arange(S)[:, None] * inv_freq[None, :]
    return np.sin(ang), np.cos(ang)


def apply_rope(x, sin, cos):
    sin2 = np.repeat(sin, 2, axis=-1)[None, :, None, :]
    cos2 = np.repeat(cos, 2, axis=-1)[None, :, None, :]
    x1 = x[..., ::2]
    x2 = x[..., 1::2]
    rot = np.stack((-x2, x1), axis=-1).reshape(x.shape)
    return x * cos2 + rot * sin2


def draw0():
    s = mx_kscale(E)
    return {"hidden_states": bf(np.random.standard_normal((B, S, E)) * s),
            "W_qkv": bf(np.random.standard_normal((3 * HD, E)) / np.sqrt(E) / s[None, :])}


def core(hidden_states, W_qkv):
    qkv = mxq(f64(hidden_states), 2, "e4m3") @ mxq(f64(W_qkv).T, 0, "e4m3")
    qkv = qkv.reshape(B, S, MP, 3 * LOC)
    q, k, v = np.split(qkv, 3, axis=-1)
    q = q.reshape(B, S, H, DH)
    k = k.reshape(B, S, H, DH)
    v = v.reshape(B, S, H, DH)
    sin, cos = rope_sincos()
    q = np.concatenate([apply_rope(q[..., :ROT], sin, cos), q[..., ROT:]], axis=-1)
    k = np.concatenate([apply_rope(k[..., :ROT], sin, cos), k[..., ROT:]], axis=-1)
    return q, k, v


def e4m3fn_bytes(y):
    return np.clip(np.asarray(y, np.float64), -448.0, 448.0).astype(np.float32).astype(ml_dtypes.float8_e4m3fn).view(np.uint8)


def e4m3fn_values(b):
    return np.asarray(b, np.uint8).view(ml_dtypes.float8_e4m3fn).astype(np.float64)


def setup_inputs():
    d = draw0()
    x0 = np.asarray(d['W_qkv']).astype(np.float64)
    s = (np.max(np.abs(x0), axis=(0,), keepdims=True) / 448.0).astype(np.float32)
    out = {}
    for k, v in d.items():
        if k == 'W_qkv':
            out['W_qkv_bytes'] = e4m3fn_bytes(x0 / s.astype(np.float64))
            out['W_qkv_scale'] = s
        else:
            out[k] = v
    return out


def reference(hidden_states, W_qkv_bytes, W_qkv_scale):
    return core(hidden_states, e4m3fn_values(W_qkv_bytes) * W_qkv_scale.astype(np.float64))

@@ -1,0 +1,256 @@
+import math
+from contextlib import ExitStack
+
+import concourse.mybir as mybir
+from concourse.masks import make_identity
+
+F32 = mybir.dt.float32
+BF16 = mybir.dt.bfloat16
+I32 = mybir.dt.int32
+U32 = mybir.dt.uint32
+U8 = mybir.dt.uint8
+FP8 = mybir.dt.float8_e4m3fn
+FP8X4 = mybir.dt.float8_e4m3fn_x4
+ALU = mybir.AluOpType
+ACT = mybir.ActivationFunctionType
+
+P = 128
+B, S, E = 2, 512, 1024
+HEADS, DH, ROT = 8, 128, 32
+GROUPS = 4
+K_PASS = 512
+PASSES = E // K_PASS
+WORDS = K_PASS // 2
+N_TILE = 512
+TILE_HEADS = N_TILE // DH
+POS_TILES = S // P
+FLOPS = 2 * B * S * E * 3 * HEADS * DH
+
+COL_TILES = ((2, 0), (0, 0), (2, 1), (0, 1), (1, 0), (1, 1))
+
+TWO_PI_HI = 6.28125
+TWO_PI_LO = 2.0 * math.pi - TWO_PI_HI
+
+LAST_PIECE = 2
+
+
+def tile_progenattention_pa_kernel(tc, hidden_states, W_qkv_bytes, W_qkv_scale, out_0, out_1, out_2):
+    nc = tc.nc
+    outs = (out_0, out_1, out_2)
+    tiles = len(COL_TILES)
+    last = tiles - 1
+
+    with ExitStack() as ctx:
+        keep = ctx.enter_context(tc.tile_pool(name="keep", bufs=1))
+        rows_pool = ctx.enter_context(tc.tile_pool(name="rows", bufs=6))
+        turned_pool = ctx.enter_context(tc.tile_pool(name="turned", bufs=2))
+        codes_pool = ctx.enter_context(tc.tile_pool(name="codes", bufs=3))
+        stage_pool = ctx.enter_context(tc.tile_pool(name="stage", bufs=6))
+        products_pool = ctx.enter_context(tc.tile_pool(name="products", bufs=2))
+        turn_psum = ctx.enter_context(tc.psum_pool(name="turn", bufs=4))
+        acc_psum = ctx.enter_context(tc.psum_pool(name="acc", bufs=4))
+        ctx.enter_context(tc.manual_schedule())
+
+        scales = keep.tile([P, E], F32, name="scales")
+        nc.sync.dma_start(out=scales[:], in_=W_qkv_scale.rearrange("o k -> (o k)").partition_broadcast(P))
+        w_view = W_qkv_bytes.rearrange("(m s h p) k -> m s p h k", m=GROUPS, s=3, h=2, p=P)
+        x_view = hidden_states.rearrange("b (c p) k -> b c p k", p=P)
+        w_bytes = {}
+        x_rows = {}
+
+        def load_w(j):
+            s, half = COL_TILES[j]
+            for part in range(2):
+                w_bytes[(j, part)] = keep.tile([P, 2, E], U8, name="w_bytes_%d_%d" % (j, part))
+                nc.sync.dma_start(out=w_bytes[(j, part)][:], in_=w_view[2 * half + part, s])
+
+        def load_x(b):
+            for c in range(POS_TILES):
+                x_rows[(b, c)] = keep.tile([P, E], BF16, name="x_rows_%d_%d" % (b, c))
+                nc.sync.dma_start(out=x_rows[(b, c)][:], in_=x_view[b, c])
+
+        load_w(0)
+        load_x(0)
+        load_w(1)
+        load_x(1)
+        for j in range(2, tiles):
+            load_w(j)
+
+        positions = keep.tile([P, POS_TILES, 2], F32, name="positions")
+        nc.gpsimd.iota(positions[:], pattern=[[P, POS_TILES], [0, 2]], base=0, channel_multiplier=1,
+                       allow_small_or_imprecise_dtypes=True)
+        identity = keep.tile([P, P], F32, name="identity")
+        make_identity(nc, identity[:])
+
+        freqs = ROT // 2
+        entries = 2 * POS_TILES * ROT
+        angles = keep.tile([P, 2, POS_TILES, freqs, 2], F32, name="angles")
+        for j in range(freqs):
+            nc.vector.tensor_scalar(out=angles[:, 0, :, j, :], in0=positions[:], scalar1=10000.0 ** (-2.0 * j / ROT),
+                                    scalar2=None, op0=ALU.mult)
+        halves = angles[:].rearrange("p a c j e -> p a (c j e)")
+        nc.vector.tensor_scalar(out=halves[:, 1, :], in0=halves[:, 0, :], scalar1=math.pi / 2.0, scalar2=None, op0=ALU.add)
+        flat = angles[:].rearrange("p a c j e -> p (a c j e)")
+        turns = keep.tile([P, entries], I32, name="turns")
+        nc.vector.tensor_scalar(out=turns[:], in0=flat, scalar1=1.0 / (2.0 * math.pi), scalar2=None, op0=ALU.mult)
+        coarse = keep.tile([P, entries], F32, name="coarse")
+        nc.vector.scalar_tensor_tensor(out=coarse[:], in0=turns[:], scalar=-TWO_PI_HI, in1=flat, op0=ALU.mult, op1=ALU.add)
+        fine = keep.tile([P, entries], F32, name="fine")
+        nc.vector.scalar_tensor_tensor(out=fine[:], in0=turns[:], scalar=-TWO_PI_LO, in1=coarse[:], op0=ALU.mult, op1=ALU.add)
+        last_turn = keep.tile([P, entries], F32, name="last_turn")
+        nc.vector.tensor_scalar(out=last_turn[:], in0=fine[:], scalar1=math.pi, scalar2=-2.0 * math.pi,
+                                op0=ALU.is_gt, op1=ALU.mult)
+        reduced = keep.tile([P, 2, POS_TILES, freqs, 2], F32, name="reduced")
+        nc.vector.tensor_tensor(out=reduced[:].rearrange("p a c j e -> p (a c j e)"), in0=fine[:], in1=last_turn[:], op=ALU.add)
+
+        tables = keep.tile([P, 2, POS_TILES, TILE_HEADS, ROT], F32, name="tables")
+        sines = tables[:, 0].rearrange("p c h (j e) -> p c h j e", e=2)
+        over_heads = [P, POS_TILES, TILE_HEADS, freqs]
+        nc.scalar.activation(out=sines[:, :, :, :, 0], in_=reduced[:, 0, :, :, 0].unsqueeze(2).to_broadcast(over_heads),
+                             func=ACT.Sin)
+        nc.scalar.activation(out=sines[:, :, :, :, 1], in_=reduced[:, 0, :, :, 1].unsqueeze(2).to_broadcast(over_heads),
+                             func=ACT.Sin, scale=-1.0)
+        nc.scalar.activation(out=tables[:, 1],
+                             in_=reduced[:, 1].rearrange("p c j e -> p c (j e)").unsqueeze(2).to_broadcast(
+                                 [P, POS_TILES, TILE_HEADS, ROT]),
+                             func=ACT.Sin)
+
+        def turn_rows(rows, words_out):
+            words = rows.bitcast(F32)
+            bank = turn_psum.tile([P, PASSES, 2, P], F32, name="bank")
+            for g in range(PASSES):
+                for u in range(2):
+                    nc.tensor.transpose(bank[:, g, u, :], words[:, WORDS * g + u: WORDS * (g + 1): 2], identity[:])
+            nc.scalar.copy(out=words_out, in_=bank[:].rearrange("p g u r -> p g r u"))
+
+        x_turned = {}
+        x_codes = {}
+        x_scales = {}
+
+        def turn_x(b, c):
+            if c == 0:
+                x_turned[b] = turned_pool.tile([P, POS_TILES * PASSES * P * 4], BF16, name="x_turned", align_bytes=64)
+            view = x_turned[b][:].bitcast(F32).rearrange("p (c g r u) -> p c g r u", c=POS_TILES, g=PASSES, u=2)
+            turn_rows(x_rows[(b, c)][:], view[:, c])
+
+        def quantize_x(b):
+            x_codes[b] = keep.tile([P, POS_TILES * PASSES * P], U32, name="x_codes_%d" % b, align_bytes=64)
+            x_scales[b] = keep.tile([P, POS_TILES * PASSES * P], U8, name="x_scales_%d" % b, align_bytes=64)
+            nc.vector.quantize_mx(out=x_codes[b][:].bitcast(FP8X4), scales=x_scales[b][:], in_=x_turned[b][:])
+
+        w_rows = {}
+        w_turned = {}
+        w_codes = {}
+        w_scales = {}
+
+        def scale_rows(j, part):
+            for h in range(2):
+                w_rows[(j, 2 * part + h)] = rows_pool.tile([P, E], BF16, name="w_rows")
+                nc.vector.tensor_tensor(out=w_rows[(j, 2 * part + h)][:], in0=w_bytes[(j, part)][:, h, :].bitcast(FP8),
+                                        in1=scales[:], op=ALU.mult)
+
+        def turn_w(j, part):
+            if part == 0:
+                w_turned[j] = turned_pool.tile([P, PASSES * N_TILE * 4], BF16, name="w_turned", align_bytes=64)
+            view = w_turned[j][:].bitcast(F32).rearrange("p (g r u) -> p g r u", g=PASSES, u=2)
+            for rt in (2 * part, 2 * part + 1):
+                turn_rows(w_rows[(j, rt)][:], view[:, :, rt * P:(rt + 1) * P, :])
+
+        def quantize_w(j):
+            w_codes[j] = codes_pool.tile([P, PASSES * N_TILE], U32, name="w_codes", align_bytes=64)
+            w_scales[j] = codes_pool.tile([P, PASSES * N_TILE], U8, name="w_scales", align_bytes=64)
+            nc.vector.quantize_mx(out=w_codes[j][:].bitcast(FP8X4), scales=w_scales[j][:], in_=w_turned[j][:])
+
+        staged = {}
+        products = {}
+
+        def rotated(j):
+            return 0 <= j < tiles and COL_TILES[j][0] < 2
+
+        def multiply(j, b):
+            staged[(j, b)] = stage_pool.tile([P, POS_TILES, N_TILE], F32, name="staged")
+            for c in range(POS_TILES):
+                acc = acc_psum.tile([P, N_TILE], F32, name="acc")
+                for g in range(PASSES):
+                    x_cols = slice((c * PASSES + g) * P, (c * PASSES + g + 1) * P)
+                    w_cols = slice(g * N_TILE, (g + 1) * N_TILE)
+                    nc.tensor.matmul_mx(
+                        out=acc[:],
+                        lhsT=x_codes[b][:, x_cols].bitcast(FP8X4),
+                        lhsT_scale=x_scales[b][:, x_cols],
+                        rhs=w_codes[j][:, w_cols].bitcast(FP8X4),
+                        rhs_scale=w_scales[j][:, w_cols],
+                        start=(g == 0),
+                        stop=(g == PASSES - 1),
+                    )
+                nc.scalar.copy(out=staged[(j, b)][:, c, :], in_=acc[:])
+
+        def store(j, b, c0, c1):
+            s, half = COL_TILES[j]
+            out_view = outs[s].rearrange("b (c p) h d -> b p c (h d)", p=P)
+            nc.sync.dma_start(out=out_view[b][:, c0:c1, half * N_TILE:(half + 1) * N_TILE], in_=staged[(j, b)][:, c0:c1, :])
+
+        def store_plain(j, b):
+            if not rotated(j):
+                store(j, b, 0, POS_TILES)
+
+        def rotary(j, b, c0, c1):
+            return staged[(j, b)][:, c0:c1, :].rearrange("p c (h f) -> p (c h) f", f=DH)[:, :, 0:ROT]
+
+        def rope_products(j, b, c0=0, c1=POS_TILES):
+            if rotated(j):
+                count = (c1 - c0) * TILE_HEADS
+                products[(j, b, c0)] = products_pool.tile([P, 2, POS_TILES * TILE_HEADS, ROT], F32, name="products")
+                nc.vector.tensor_tensor(out=products[(j, b, c0)][:, :, 0:count, :],
+                                        in0=rotary(j, b, c0, c1).unsqueeze(1).to_broadcast([P, 2, count, ROT]),
+                                        in1=tables[:, :, c0:c1].rearrange("p v c h f -> p v (c h) f"), op=ALU.mult)
+
+        def rope_sum(j, b, c0=0, c1=POS_TILES):
+            if rotated(j):
+                count = (c1 - c0) * TILE_HEADS
+                by_sin = products[(j, b, c0)][:, 0, 0:count, :].rearrange("p a (j e) -> p a j e", e=2)
+                by_cos = products[(j, b, c0)][:, 1, 0:count, :].rearrange("p a (j e) -> p a j e", e=2)
+                nc.vector.tensor_tensor(out=rotary(j, b, c0, c1).rearrange("p a (j e) -> p a j e", e=2),
+                                        in0=by_cos, in1=by_sin[:, :, :, ::-1], op=ALU.add)
+                store(j, b, c0, c1)
+
+        for part in range(2):
+            scale_rows(0, part)
+            turn_w(0, part)
+            turn_x(0, 2 * part)
+            turn_x(0, 2 * part + 1)
+        scale_rows(1, 0)
+        for c in range(POS_TILES):
+            turn_x(1, c)
+        quantize_w(0)
+        quantize_x(0)
+        turn_w(1, 0)
+        quantize_x(1)
+
+        for n in range(1, tiles):
+            m, r = n - 1, n - 2
+            multiply(m, 0)
+            store_plain(m, 0)
+            scale_rows(n, 1)
+            rope_sum(r, 0)
+            turn_w(n, 1)
+            multiply(m, 1)
+            store_plain(m, 1)
+            rope_products(r, 1)
+            if n < last:
+                scale_rows(n + 1, 0)
+            rope_sum(r, 1)
+            rope_products(m, 0)
+            quantize_w(n)
+            if n < last:
+                turn_w(n + 1, 0)
+
+        multiply(last, 0)
+        rope_sum(last - 1, 0)
+        multiply(last, 1)
+        rope_products(last - 1, 1)
+        rope_sum(last - 1, 1)
+        for b in range(B):
+            for c0 in range(0, POS_TILES, LAST_PIECE):
+                rope_products(last, b, c0, c0 + LAST_PIECE)
+                rope_sum(last, b, c0, c0 + LAST_PIECE)

@@ -58,23 +58,28 @@ def tile_progenattention_pa_kernel(tc, hidden_states, W_qkv_bytes, W_qkv_scale, 
         w_bytes = {}
         x_rows = {}
 
-        def load_w(j):
+        def load_w(j, part):
             s, half = COL_TILES[j]
-            for part in range(2):
-                w_bytes[(j, part)] = keep.tile([P, 2, E], U8, name="w_bytes_%d_%d" % (j, part))
-                nc.sync.dma_start(out=w_bytes[(j, part)][:], in_=w_view[2 * half + part, s])
+            w_bytes[(j, part)] = keep.tile([P, 2, E], U8, name="w_bytes_%d_%d" % (j, part))
+            nc.sync.dma_start(out=w_bytes[(j, part)][:], in_=w_view[2 * half + part, s])
 
-        def load_x(b):
-            for c in range(POS_TILES):
-                x_rows[(b, c)] = keep.tile([P, E], BF16, name="x_rows_%d_%d" % (b, c))
-                nc.sync.dma_start(out=x_rows[(b, c)][:], in_=x_view[b, c])
+        def load_x(b, c):
+            x_rows[(b, c)] = keep.tile([P, E], BF16, name="x_rows_%d_%d" % (b, c))
+            nc.sync.dma_start(out=x_rows[(b, c)][:], in_=x_view[b, c])
 
-        load_w(0)
-        load_x(0)
-        load_w(1)
-        load_x(1)
+        load_w(0, 0)
+        load_x(0, 0)
+        load_x(0, 1)
+        load_w(0, 1)
+        load_x(0, 2)
+        load_x(0, 3)
+        load_w(1, 0)
+        load_w(1, 1)
+        for c in range(POS_TILES):
+            load_x(1, c)
         for j in range(2, tiles):
-            load_w(j)
+            load_w(j, 0)
+            load_w(j, 1)
 
         positions = keep.tile([P, POS_TILES, 2], F32, name="positions")
         nc.gpsimd.iota(positions[:], pattern=[[P, POS_TILES], [0, 2]], base=0, channel_multiplier=1,
@@ -149,12 +154,15 @@ def tile_progenattention_pa_kernel(tc, hidden_states, W_qkv_bytes, W_qkv_scale, 
                 nc.vector.tensor_tensor(out=w_rows[(j, 2 * part + h)][:], in0=w_bytes[(j, part)][:, h, :].bitcast(FP8),
                                         in1=scales[:], op=ALU.mult)
 
-        def turn_w(j, part):
-            if part == 0:
+        def turn_w_rows(j, rt):
+            if rt == 0:
                 w_turned[j] = turned_pool.tile([P, PASSES * N_TILE * 4], BF16, name="w_turned", align_bytes=64)
             view = w_turned[j][:].bitcast(F32).rearrange("p (g r u) -> p g r u", g=PASSES, u=2)
-            for rt in (2 * part, 2 * part + 1):
-                turn_rows(w_rows[(j, rt)][:], view[:, :, rt * P:(rt + 1) * P, :])
+            turn_rows(w_rows[(j, rt)][:], view[:, :, rt * P:(rt + 1) * P, :])
+
+        def turn_w(j, part):
+            turn_w_rows(j, 2 * part)
+            turn_w_rows(j, 2 * part + 1)
 
         def quantize_w(j):
             w_codes[j] = codes_pool.tile([P, PASSES * N_TILE], U32, name="w_codes", align_bytes=64)
@@ -214,41 +222,56 @@ def tile_progenattention_pa_kernel(tc, hidden_states, W_qkv_bytes, W_qkv_scale, 
                                         in0=by_cos, in1=by_sin[:, :, :, ::-1], op=ALU.add)
                 store(j, b, c0, c1)
 
-        for part in range(2):
-            scale_rows(0, part)
-            turn_w(0, part)
-            turn_x(0, 2 * part)
-            turn_x(0, 2 * part + 1)
+        scale_rows(0, 0)
+        turn_x(0, 0)
+        turn_w_rows(0, 0)
+        turn_x(0, 1)
+        turn_w_rows(0, 1)
+        scale_rows(0, 1)
+        turn_x(0, 2)
+        turn_x(0, 3)
+        turn_w_rows(0, 2)
+        turn_w_rows(0, 3)
         scale_rows(1, 0)
-        for c in range(POS_TILES):
-            turn_x(1, c)
+        turn_x(1, 0)
+        turn_x(1, 1)
+        turn_w_rows(1, 0)
+        turn_x(1, 2)
+        turn_x(1, 3)
+        turn_w_rows(1, 1)
+        scale_rows(1, 1)
+        turn_w(1, 1)
         quantize_w(0)
         quantize_x(0)
-        turn_w(1, 0)
         quantize_x(1)
 
-        for n in range(1, tiles):
+        for n in range(1, last):
             m, r = n - 1, n - 2
+            rope_sum(r, 0)
             multiply(m, 0)
             store_plain(m, 0)
-            scale_rows(n, 1)
-            rope_sum(r, 0)
-            turn_w(n, 1)
+            rope_products(r, 1)
+            scale_rows(n + 1, 0)
+            rope_sum(r, 1)
             multiply(m, 1)
             store_plain(m, 1)
-            rope_products(r, 1)
-            if n < last:
-                scale_rows(n + 1, 0)
-            rope_sum(r, 1)
+            scale_rows(n + 1, 1)
+            turn_w(n + 1, 0)
+            turn_w(n + 1, 1)
             rope_products(m, 0)
             quantize_w(n)
-            if n < last:
-                turn_w(n + 1, 0)
 
+        rope_sum(last - 2, 0)
+        multiply(last - 1, 0)
+        rope_products(last - 2, 1)
+        rope_sum(last - 2, 1)
+        quantize_w(last)
+        multiply(last - 1, 1)
+        rope_products(last - 1, 0)
         multiply(last, 0)
         rope_sum(last - 1, 0)
-        multiply(last, 1)
         rope_products(last - 1, 1)
+        multiply(last, 1)
         rope_sum(last - 1, 1)
         for b in range(B):
             for c0 in range(0, POS_TILES, LAST_PIECE):

@@ -52,7 +52,7 @@ def tile_progenattention_pa_kernel(tc, hidden_states, W_qkv_bytes, W_qkv_scale, 
         ctx.enter_context(tc.manual_schedule())
 
         scales = keep.tile([P, E], F32, name="scales")
-        nc.sync.dma_start(out=scales[:], in_=W_qkv_scale.rearrange("o k -> (o k)").partition_broadcast(P))
+        nc.scalar.dma_start(out=scales[:], in_=W_qkv_scale.rearrange("o k -> (o k)").partition_broadcast(P))
         w_view = W_qkv_bytes.rearrange("(m s h p) k -> m s p h k", m=GROUPS, s=3, h=2, p=P)
         x_view = hidden_states.rearrange("b (c p) k -> b c p k", p=P)
         w_bytes = {}

@@ -46,7 +46,7 @@ def tile_progenattention_pa_kernel(tc, hidden_states, W_qkv_bytes, W_qkv_scale, 
         turned_pool = ctx.enter_context(tc.tile_pool(name="turned", bufs=2))
         codes_pool = ctx.enter_context(tc.tile_pool(name="codes", bufs=3))
         stage_pool = ctx.enter_context(tc.tile_pool(name="stage", bufs=6))
-        products_pool = ctx.enter_context(tc.tile_pool(name="products", bufs=2))
+        products_pool = ctx.enter_context(tc.tile_pool(name="products", bufs=3))
         turn_psum = ctx.enter_context(tc.psum_pool(name="turn", bufs=4))
         acc_psum = ctx.enter_context(tc.psum_pool(name="acc", bufs=4))
         ctx.enter_context(tc.manual_schedule())
@@ -81,21 +81,21 @@ def tile_progenattention_pa_kernel(tc, hidden_states, W_qkv_bytes, W_qkv_scale, 
             load_w(j, 0)
             load_w(j, 1)
 
-        positions = keep.tile([P, POS_TILES, 2], F32, name="positions")
-        nc.gpsimd.iota(positions[:], pattern=[[P, POS_TILES], [0, 2]], base=0, channel_multiplier=1,
+        positions = keep.tile([P, POS_TILES], F32, name="positions")
+        nc.gpsimd.iota(positions[:], pattern=[[P, POS_TILES]], base=0, channel_multiplier=1,
                        allow_small_or_imprecise_dtypes=True)
         identity = keep.tile([P, P], F32, name="identity")
         make_identity(nc, identity[:])
 
         freqs = ROT // 2
-        entries = 2 * POS_TILES * ROT
-        angles = keep.tile([P, 2, POS_TILES, freqs, 2], F32, name="angles")
+        entries = 2 * POS_TILES * freqs
+        angles = keep.tile([P, 2, POS_TILES, freqs], F32, name="angles")
         for j in range(freqs):
-            nc.vector.tensor_scalar(out=angles[:, 0, :, j, :], in0=positions[:], scalar1=10000.0 ** (-2.0 * j / ROT),
+            nc.vector.tensor_scalar(out=angles[:, 0, :, j], in0=positions[:], scalar1=10000.0 ** (-2.0 * j / ROT),
                                     scalar2=None, op0=ALU.mult)
-        halves = angles[:].rearrange("p a c j e -> p a (c j e)")
+        halves = angles[:].rearrange("p a c j -> p a (c j)")
         nc.vector.tensor_scalar(out=halves[:, 1, :], in0=halves[:, 0, :], scalar1=math.pi / 2.0, scalar2=None, op0=ALU.add)
-        flat = angles[:].rearrange("p a c j e -> p (a c j e)")
+        flat = angles[:].rearrange("p a c j -> p (a c j)")
         turns = keep.tile([P, entries], I32, name="turns")
         nc.vector.tensor_scalar(out=turns[:], in0=flat, scalar1=1.0 / (2.0 * math.pi), scalar2=None, op0=ALU.mult)
         coarse = keep.tile([P, entries], F32, name="coarse")
@@ -105,20 +105,16 @@ def tile_progenattention_pa_kernel(tc, hidden_states, W_qkv_bytes, W_qkv_scale, 
         last_turn = keep.tile([P, entries], F32, name="last_turn")
         nc.vector.tensor_scalar(out=last_turn[:], in0=fine[:], scalar1=math.pi, scalar2=-2.0 * math.pi,
                                 op0=ALU.is_gt, op1=ALU.mult)
-        reduced = keep.tile([P, 2, POS_TILES, freqs, 2], F32, name="reduced")
-        nc.vector.tensor_tensor(out=reduced[:].rearrange("p a c j e -> p (a c j e)"), in0=fine[:], in1=last_turn[:], op=ALU.add)
+        reduced = keep.tile([P, 2, POS_TILES, freqs], F32, name="reduced")
+        nc.vector.tensor_tensor(out=reduced[:].rearrange("p a c j -> p (a c j)"), in0=fine[:], in1=last_turn[:], op=ALU.add)
 
         tables = keep.tile([P, 2, POS_TILES, TILE_HEADS, ROT], F32, name="tables")
-        sines = tables[:, 0].rearrange("p c h (j e) -> p c h j e", e=2)
         over_heads = [P, POS_TILES, TILE_HEADS, freqs]
-        nc.scalar.activation(out=sines[:, :, :, :, 0], in_=reduced[:, 0, :, :, 0].unsqueeze(2).to_broadcast(over_heads),
-                             func=ACT.Sin)
-        nc.scalar.activation(out=sines[:, :, :, :, 1], in_=reduced[:, 0, :, :, 1].unsqueeze(2).to_broadcast(over_heads),
-                             func=ACT.Sin, scale=-1.0)
-        nc.scalar.activation(out=tables[:, 1],
-                             in_=reduced[:, 1].rearrange("p c j e -> p c (j e)").unsqueeze(2).to_broadcast(
-                                 [P, POS_TILES, TILE_HEADS, ROT]),
-                             func=ACT.Sin)
+        for v in range(2):
+            pairs = tables[:, v].rearrange("p c h (j e) -> p c h j e", e=2)
+            for e in range(2):
+                nc.scalar.activation(out=pairs[:, :, :, :, e], in_=reduced[:, v].unsqueeze(2).to_broadcast(over_heads),
+                                     func=ACT.Sin, scale=(-1.0 if (v == 0 and e == 1) else 1.0))
 
         def turn_rows(rows, words_out):
             words = rows.bitcast(F32)
@@ -261,19 +257,24 @@ def tile_progenattention_pa_kernel(tc, hidden_states, W_qkv_bytes, W_qkv_scale, 
             rope_products(m, 0)
             quantize_w(n)
 
+        pieces = [(j, b, c0) for j in (last - 1, last) for b in range(B) for c0 in range(0, POS_TILES, LAST_PIECE)]
+
+        def piece_products(i):
+            rope_products(pieces[i][0], pieces[i][1], pieces[i][2], pieces[i][2] + LAST_PIECE)
+
+        def piece_sum(i):
+            rope_sum(pieces[i][0], pieces[i][1], pieces[i][2], pieces[i][2] + LAST_PIECE)
+
         rope_sum(last - 2, 0)
         multiply(last - 1, 0)
         rope_products(last - 2, 1)
         rope_sum(last - 2, 1)
+        piece_products(0)
         quantize_w(last)
         multiply(last - 1, 1)
-        rope_products(last - 1, 0)
         multiply(last, 0)
-        rope_sum(last - 1, 0)
-        rope_products(last - 1, 1)
         multiply(last, 1)
-        rope_sum(last - 1, 1)
-        for b in range(B):
-            for c0 in range(0, POS_TILES, LAST_PIECE):
-                rope_products(last, b, c0, c0 + LAST_PIECE)
-                rope_sum(last, b, c0, c0 + LAST_PIECE)
+        for i in range(1, len(pieces)):
+            piece_products(i)
+            piece_sum(i - 1)
+        piece_sum(len(pieces) - 1)

import math
from contextlib import ExitStack

import concourse.mybir as mybir
from concourse.masks import make_identity

F32 = mybir.dt.float32
BF16 = mybir.dt.bfloat16
I32 = mybir.dt.int32
U32 = mybir.dt.uint32
U8 = mybir.dt.uint8
FP8 = mybir.dt.float8_e4m3fn
FP8X4 = mybir.dt.float8_e4m3fn_x4
ALU = mybir.AluOpType
ACT = mybir.ActivationFunctionType

P = 128
B, S, E = 2, 512, 1024
HEADS, DH, ROT = 8, 128, 32
GROUPS = 4
K_PASS = 512
PASSES = E // K_PASS
WORDS = K_PASS // 2
N_TILE = 512
TILE_HEADS = N_TILE // DH
POS_TILES = S // P
FLOPS = 2 * B * S * E * 3 * HEADS * DH

COL_TILES = ((2, 0), (0, 0), (2, 1), (0, 1), (1, 0), (1, 1))

TWO_PI_HI = 6.28125
TWO_PI_LO = 2.0 * math.pi - TWO_PI_HI

LAST_PIECE = 2


def tile_progenattention_pa_kernel(tc, hidden_states, W_qkv_bytes, W_qkv_scale, out_0, out_1, out_2):
    nc = tc.nc
    outs = (out_0, out_1, out_2)
    tiles = len(COL_TILES)
    last = tiles - 1

    with ExitStack() as ctx:
        keep = ctx.enter_context(tc.tile_pool(name="keep", bufs=1))
        rows_pool = ctx.enter_context(tc.tile_pool(name="rows", bufs=6))
        turned_pool = ctx.enter_context(tc.tile_pool(name="turned", bufs=2))
        codes_pool = ctx.enter_context(tc.tile_pool(name="codes", bufs=3))
        stage_pool = ctx.enter_context(tc.tile_pool(name="stage", bufs=6))
        products_pool = ctx.enter_context(tc.tile_pool(name="products", bufs=3))
        turn_psum = ctx.enter_context(tc.psum_pool(name="turn", bufs=4))
        acc_psum = ctx.enter_context(tc.psum_pool(name="acc", bufs=4))
        ctx.enter_context(tc.manual_schedule())

        scales = keep.tile([P, E], F32, name="scales")
        nc.scalar.dma_start(out=scales[:], in_=W_qkv_scale.rearrange("o k -> (o k)").partition_broadcast(P))
        w_view = W_qkv_bytes.rearrange("(m s h p) k -> m s p h k", m=GROUPS, s=3, h=2, p=P)
        x_view = hidden_states.rearrange("b (c p) k -> b c p k", p=P)
        w_bytes = {}
        x_rows = {}

        def load_w(j, part):
            s, half = COL_TILES[j]
            w_bytes[(j, part)] = keep.tile([P, 2, E], U8, name="w_bytes_%d_%d" % (j, part))
            nc.sync.dma_start(out=w_bytes[(j, part)][:], in_=w_view[2 * half + part, s])

        def load_x(b, c):
            x_rows[(b, c)] = keep.tile([P, E], BF16, name="x_rows_%d_%d" % (b, c))
            nc.sync.dma_start(out=x_rows[(b, c)][:], in_=x_view[b, c])

        load_w(0, 0)
        load_x(0, 0)
        load_x(0, 1)
        load_w(0, 1)
        load_x(0, 2)
        load_x(0, 3)
        load_w(1, 0)
        load_w(1, 1)
        for c in range(POS_TILES):
            load_x(1, c)
        for j in range(2, tiles):
            load_w(j, 0)
            load_w(j, 1)

        positions = keep.tile([P, POS_TILES], F32, name="positions")
        nc.gpsimd.iota(positions[:], pattern=[[P, POS_TILES]], base=0, channel_multiplier=1,
                       allow_small_or_imprecise_dtypes=True)
        identity = keep.tile([P, P], F32, name="identity")
        make_identity(nc, identity[:])

        freqs = ROT // 2
        entries = 2 * POS_TILES * freqs
        angles = keep.tile([P, 2, POS_TILES, freqs], F32, name="angles")
        for j in range(freqs):
            nc.vector.tensor_scalar(out=angles[:, 0, :, j], in0=positions[:], scalar1=10000.0 ** (-2.0 * j / ROT),
                                    scalar2=None, op0=ALU.mult)
        halves = angles[:].rearrange("p a c j -> p a (c j)")
        nc.vector.tensor_scalar(out=halves[:, 1, :], in0=halves[:, 0, :], scalar1=math.pi / 2.0, scalar2=None, op0=ALU.add)
        flat = angles[:].rearrange("p a c j -> p (a c j)")
        turns = keep.tile([P, entries], I32, name="turns")
        nc.vector.tensor_scalar(out=turns[:], in0=flat, scalar1=1.0 / (2.0 * math.pi), scalar2=None, op0=ALU.mult)
        coarse = keep.tile([P, entries], F32, name="coarse")
        nc.vector.scalar_tensor_tensor(out=coarse[:], in0=turns[:], scalar=-TWO_PI_HI, in1=flat, op0=ALU.mult, op1=ALU.add)
        fine = keep.tile([P, entries], F32, name="fine")
        nc.vector.scalar_tensor_tensor(out=fine[:], in0=turns[:], scalar=-TWO_PI_LO, in1=coarse[:], op0=ALU.mult, op1=ALU.add)
        last_turn = keep.tile([P, entries], F32, name="last_turn")
        nc.vector.tensor_scalar(out=last_turn[:], in0=fine[:], scalar1=math.pi, scalar2=-2.0 * math.pi,
                                op0=ALU.is_gt, op1=ALU.mult)
        reduced = keep.tile([P, 2, POS_TILES, freqs], F32, name="reduced")
        nc.vector.tensor_tensor(out=reduced[:].rearrange("p a c j -> p (a c j)"), in0=fine[:], in1=last_turn[:], op=ALU.add)

        tables = keep.tile([P, 2, POS_TILES, TILE_HEADS, ROT], F32, name="tables")
        over_heads = [P, POS_TILES, TILE_HEADS, freqs]
        for v in range(2):
            pairs = tables[:, v].rearrange("p c h (j e) -> p c h j e", e=2)
            for e in range(2):
                nc.scalar.activation(out=pairs[:, :, :, :, e], in_=reduced[:, v].unsqueeze(2).to_broadcast(over_heads),
                                     func=ACT.Sin, scale=(-1.0 if (v == 0 and e == 1) else 1.0))

        def turn_rows(rows, words_out):
            words = rows.bitcast(F32)
            bank = turn_psum.tile([P, PASSES, 2, P], F32, name="bank")
            for g in range(PASSES):
                for u in range(2):
                    nc.tensor.transpose(bank[:, g, u, :], words[:, WORDS * g + u: WORDS * (g + 1): 2], identity[:])
            nc.scalar.copy(out=words_out, in_=bank[:].rearrange("p g u r -> p g r u"))

        x_turned = {}
        x_codes = {}
        x_scales = {}

        def turn_x(b, c):
            if c == 0:
                x_turned[b] = turned_pool.tile([P, POS_TILES * PASSES * P * 4], BF16, name="x_turned", align_bytes=64)
            view = x_turned[b][:].bitcast(F32).rearrange("p (c g r u) -> p c g r u", c=POS_TILES, g=PASSES, u=2)
            turn_rows(x_rows[(b, c)][:], view[:, c])

        def quantize_x(b):
            x_codes[b] = keep.tile([P, POS_TILES * PASSES * P], U32, name="x_codes_%d" % b, align_bytes=64)
            x_scales[b] = keep.tile([P, POS_TILES * PASSES * P], U8, name="x_scales_%d" % b, align_bytes=64)
            nc.vector.quantize_mx(out=x_codes[b][:].bitcast(FP8X4), scales=x_scales[b][:], in_=x_turned[b][:])

        w_rows = {}
        w_turned = {}
        w_codes = {}
        w_scales = {}

        def scale_rows(j, part):
            for h in range(2):
                w_rows[(j, 2 * part + h)] = rows_pool.tile([P, E], BF16, name="w_rows")
                nc.vector.tensor_tensor(out=w_rows[(j, 2 * part + h)][:], in0=w_bytes[(j, part)][:, h, :].bitcast(FP8),
                                        in1=scales[:], op=ALU.mult)

        def turn_w_rows(j, rt):
            if rt == 0:
                w_turned[j] = turned_pool.tile([P, PASSES * N_TILE * 4], BF16, name="w_turned", align_bytes=64)
            view = w_turned[j][:].bitcast(F32).rearrange("p (g r u) -> p g r u", g=PASSES, u=2)
            turn_rows(w_rows[(j, rt)][:], view[:, :, rt * P:(rt + 1) * P, :])

        def turn_w(j, part):
            turn_w_rows(j, 2 * part)
            turn_w_rows(j, 2 * part + 1)

        def quantize_w(j):
            w_codes[j] = codes_pool.tile([P, PASSES * N_TILE], U32, name="w_codes", align_bytes=64)
            w_scales[j] = codes_pool.tile([P, PASSES * N_TILE], U8, name="w_scales", align_bytes=64)
            nc.vector.quantize_mx(out=w_codes[j][:].bitcast(FP8X4), scales=w_scales[j][:], in_=w_turned[j][:])

        staged = {}
        products = {}

        def rotated(j):
            return 0 <= j < tiles and COL_TILES[j][0] < 2

        def multiply(j, b):
            staged[(j, b)] = stage_pool.tile([P, POS_TILES, N_TILE], F32, name="staged")
            for c in range(POS_TILES):
                acc = acc_psum.tile([P, N_TILE], F32, name="acc")
                for g in range(PASSES):
                    x_cols = slice((c * PASSES + g) * P, (c * PASSES + g + 1) * P)
                    w_cols = slice(g * N_TILE, (g + 1) * N_TILE)
                    nc.tensor.matmul_mx(
                        out=acc[:],
                        lhsT=x_codes[b][:, x_cols].bitcast(FP8X4),
                        lhsT_scale=x_scales[b][:, x_cols],
                        rhs=w_codes[j][:, w_cols].bitcast(FP8X4),
                        rhs_scale=w_scales[j][:, w_cols],
                        start=(g == 0),
                        stop=(g == PASSES - 1),
                    )
                nc.scalar.copy(out=staged[(j, b)][:, c, :], in_=acc[:])

        def store(j, b, c0, c1):
            s, half = COL_TILES[j]
            out_view = outs[s].rearrange("b (c p) h d -> b p c (h d)", p=P)
            nc.sync.dma_start(out=out_view[b][:, c0:c1, half * N_TILE:(half + 1) * N_TILE], in_=staged[(j, b)][:, c0:c1, :])

        def store_plain(j, b):
            if not rotated(j):
                store(j, b, 0, POS_TILES)

        def rotary(j, b, c0, c1):
            return staged[(j, b)][:, c0:c1, :].rearrange("p c (h f) -> p (c h) f", f=DH)[:, :, 0:ROT]

        def rope_products(j, b, c0=0, c1=POS_TILES):
            if rotated(j):
                count = (c1 - c0) * TILE_HEADS
                products[(j, b, c0)] = products_pool.tile([P, 2, POS_TILES * TILE_HEADS, ROT], F32, name="products")
                nc.vector.tensor_tensor(out=products[(j, b, c0)][:, :, 0:count, :],
                                        in0=rotary(j, b, c0, c1).unsqueeze(1).to_broadcast([P, 2, count, ROT]),
                                        in1=tables[:, :, c0:c1].rearrange("p v c h f -> p v (c h) f"), op=ALU.mult)

        def rope_sum(j, b, c0=0, c1=POS_TILES):
            if rotated(j):
                count = (c1 - c0) * TILE_HEADS
                by_sin = products[(j, b, c0)][:, 0, 0:count, :].rearrange("p a (j e) -> p a j e", e=2)
                by_cos = products[(j, b, c0)][:, 1, 0:count, :].rearrange("p a (j e) -> p a j e", e=2)
                nc.vector.tensor_tensor(out=rotary(j, b, c0, c1).rearrange("p a (j e) -> p a j e", e=2),
                                        in0=by_cos, in1=by_sin[:, :, :, ::-1], op=ALU.add)
                store(j, b, c0, c1)

        scale_rows(0, 0)
        turn_x(0, 0)
        turn_w_rows(0, 0)
        turn_x(0, 1)
        turn_w_rows(0, 1)
        scale_rows(0, 1)
        turn_x(0, 2)
        turn_x(0, 3)
        turn_w_rows(0, 2)
        turn_w_rows(0, 3)
        scale_rows(1, 0)
        turn_x(1, 0)
        turn_x(1, 1)
        turn_w_rows(1, 0)
        turn_x(1, 2)
        turn_x(1, 3)
        turn_w_rows(1, 1)
        scale_rows(1, 1)
        turn_w(1, 1)
        quantize_w(0)
        quantize_x(0)
        quantize_x(1)

        for n in range(1, last):
            m, r = n - 1, n - 2
            rope_sum(r, 0)
            multiply(m, 0)
            store_plain(m, 0)
            rope_products(r, 1)
            scale_rows(n + 1, 0)
            rope_sum(r, 1)
            multiply(m, 1)
            store_plain(m, 1)
            scale_rows(n + 1, 1)
            turn_w(n + 1, 0)
            turn_w(n + 1, 1)
            rope_products(m, 0)
            quantize_w(n)

        pieces = [(j, b, c0) for j in (last - 1, last) for b in range(B) for c0 in range(0, POS_TILES, LAST_PIECE)]

        def piece_products(i):
            rope_products(pieces[i][0], pieces[i][1], pieces[i][2], pieces[i][2] + LAST_PIECE)

        def piece_sum(i):
            rope_sum(pieces[i][0], pieces[i][1], pieces[i][2], pieces[i][2] + LAST_PIECE)

        rope_sum(last - 2, 0)
        multiply(last - 1, 0)
        rope_products(last - 2, 1)
        rope_sum(last - 2, 1)
        piece_products(0)
        quantize_w(last)
        multiply(last - 1, 1)
        multiply(last, 0)
        multiply(last, 1)
        for i in range(1, len(pieces)):
            piece_products(i)
            piece_sum(i - 1)
        piece_sum(len(pieces) - 1)
